import numpy as np
import ml_dtypes


def mxq(x, axis, fmt="e4m3"):
    dtype, down = {"e4m3": (ml_dtypes.float8_e4m3fn, 7), "e5m2": (ml_dtypes.float8_e5m2, 14)}[fmt]
    v = np.moveaxis(np.asarray(x, np.float32).astype(ml_dtypes.bfloat16).astype(np.float64), axis, -1)
    blocks = v.reshape(v.shape[:-1] + (-1, 32))
    amax = np.abs(blocks).max(-1, keepdims=True)
    byte = np.maximum(np.where(amax > 0, np.frexp(amax)[1] - 1 + 127, 0) - down, 1)
    scale = np.exp2(byte - 127.0)
    codes = (blocks / scale).astype(np.float32).astype(dtype).astype(np.float64)
    return np.moveaxis((codes * scale).reshape(v.shape), -1, axis)


WIDE = False


def mx_kscale(k):
    if not WIDE:
        return np.ones(k)
    levels = np.array([10, -10, 5, -5, 0])
    if k % 512:
        return np.exp2(np.random.permutation(np.resize(levels, k // 32))).repeat(32)
    a = np.empty((k // 512, 16))
    for p in range(k // 512):
        a[p, :8] = np.random.permutation(np.resize(levels, 8))
        for g in range(8):
            far = levels[np.abs(levels - a[p, g]) >= 10]
            a[p, g + 8] = far[np.random.randint(len(far))]
    return np.exp2(a.ravel()).repeat(32)


BF16 = ml_dtypes.bfloat16


def bf(x):
    return np.asarray(x, np.float32).astype(BF16)


def f64(x):
    return np.asarray(x).astype(np.float64)


B, S, HIDDEN, HEADS, BLK = 1, 2048, 1024, 8, 512
HEAD = HIDDEN // HEADS


def gammas():
    return 1.0 - np.exp(np.log(2.0) * np.linspace(-9.0, -5.0, HEADS))


def decay(lo, hi):
    diff = np.arange(lo, hi)[:, None] - np.arange(hi)[None, :]
    causal = diff >= 0
    safe = np.where(causal, diff, 0)
    return np.where(causal[None], gammas()[:, None, None] ** safe[None], 0.0)


def setup_inputs():
    s = mx_kscale(S)[None, :, None, None]
    return {"q": bf(np.random.standard_normal((B, S, HEADS, HEAD)) * HEAD ** -0.25),
            "k": bf(np.random.standard_normal((B, S, HEADS, HEAD)) * HEAD ** -0.25 * s),
            "v": bf(np.random.standard_normal((B, S, HEADS, HEAD)) * 0.3 / s)}


def reference(q, k, v):
    qh = f64(q).transpose(0, 2, 1, 3)
    kh = f64(k).transpose(0, 2, 1, 3)
    vq = mxq(f64(v).transpose(0, 2, 1, 3), 2, "e4m3")
    outs = []
    for i in range(S // BLK):
        lo, hi = i * BLK, (i + 1) * BLK
        sc = (qh[:, :, lo:hi] @ kh[:, :, :hi].transpose(0, 1, 3, 2)) * decay(lo, hi)[None]
        outs.append(mxq(sc, 3, "e4m3") @ vq[:, :, :hi])
    return np.concatenate(outs, axis=2).transpose(0, 2, 1, 3)

@@ -1,0 +1,238 @@
+import math
+from contextlib import ExitStack
+
+import concourse.mybir as mybir
+from concourse.masks import make_identity
+
+BF16 = mybir.dt.bfloat16
+F32 = mybir.dt.float32
+U32 = mybir.dt.uint32
+U8 = mybir.dt.uint8
+FP8X4 = mybir.dt.float8_e4m3fn_x4
+ALU = mybir.AluOpType
+ACT = mybir.ActivationFunctionType
+
+SEQ = 2048
+HEADS = 8
+HEAD = 128
+P = 128
+PACK = 4
+SPAN = P * PACK
+N_SPANS = SEQ // SPAN
+CELLS = 4
+LOAD_HEADS = 4
+AHEAD = 2
+WINDOW = SPAN + P
+LAG = 2
+FAR = 1.0e6
+
+FLOPS = 2 * 2 * HEAD * HEADS * SPAN * SPAN * (1 + 2 + 3 + 4)
+
+
+def tile_multiscaleretention_pa_kernel(tc, q, k, v, out):
+    nc = tc.nc
+    q_rows = q.rearrange("b s h d -> (b s) (h d)")
+    k_rows = k.rearrange("b s h d -> (b s) (h d)")
+    v_rows = v.rearrange("b s h d -> (b s) (h d)")
+    out_rows = out.rearrange("b s h d -> (b s) (h d)")
+    gammas = [1.0 - 2.0 ** (-9.0 + 4.0 * h / 7.0) for h in range(HEADS)]
+
+    jobs = [(i, h) for i in range(N_SPANS) for h in range(HEADS)]
+    rounds = []
+    for i, h in jobs:
+        rounds.append((i, h, [(r, i) for r in range(PACK)]))
+        below = [(r, j) for r in range(PACK) for j in range(i)]
+        for first in range(0, len(below), CELLS):
+            rounds.append((i, h, below[first : first + CELLS]))
+
+    with ExitStack() as stack:
+        keep = stack.enter_context(tc.tile_pool(name="keep", bufs=1))
+        raw = stack.enter_context(tc.tile_pool(name="raw", bufs=2 * HEADS // LOAD_HEADS))
+        work = stack.enter_context(tc.tile_pool(name="work", bufs=3))
+        psum_flip = stack.enter_context(tc.psum_pool(name="psum_flip", bufs=2))
+        psum_cell = stack.enter_context(tc.psum_pool(name="psum_cell", bufs=CELLS))
+        psum_out = stack.enter_context(tc.psum_pool(name="psum_out", bufs=2))
+        stack.enter_context(tc.manual_schedule())
+
+        steps = keep.tile([P, WINDOW, PACK], F32)
+        identity = keep.tile([P, P], BF16)
+        nc.gpsimd.iota(
+            out=steps[:],
+            pattern=[[1, WINDOW], [-1, PACK]],
+            base=0,
+            channel_multiplier=-PACK,
+            allow_small_or_imprecise_dtypes=True,
+        )
+        masked = steps[:, 0:SPAN]
+        nc.vector.scalar_tensor_tensor(out=masked, in0=masked, scalar=-FAR, in1=masked, op0=ALU.mult, op1=ALU.max)
+        make_identity(nc, identity[:])
+
+        q_raw, k_raw, v_raw = {}, {}, {}
+        keys_t, v_codes, v_scales = {}, {}, {}
+        decay = {}
+        queries_t, v_grouped, products, opening = {}, {}, {}, {}
+        banks, grouped, codes, scales = {}, {}, {}, {}
+        scaled = {}
+
+        def load_span(i):
+            rows = slice(i * SPAN, (i + 1) * SPAN)
+            for part in range(HEADS // LOAD_HEADS):
+                cols = slice(part * LOAD_HEADS * HEAD, (part + 1) * LOAD_HEADS * HEAD)
+                k_in = raw.tile([P, PACK, LOAD_HEADS * HEAD], BF16)
+                nc.sync.dma_start(out=k_in[:], in_=k_rows[rows, cols].rearrange("(p t) c -> p t c", t=PACK))
+                q_in = raw.tile([P, PACK, LOAD_HEADS * HEAD], BF16)
+                nc.sync.dma_start(out=q_in[:], in_=q_rows[rows, cols].rearrange("(t p) c -> p t c", p=P))
+                v_in = raw.tile([P, PACK, LOAD_HEADS * HEAD], BF16)
+                nc.sync.dma_start(out=v_in[:], in_=v_rows[rows, cols].rearrange("(p t) c -> p t c", t=PACK))
+                k_raw[(i, part)], q_raw[(i, part)], v_raw[(i, part)] = k_in, q_in, v_in
+            keys_t[i] = keep.tile([P, HEADS, PACK, P], BF16, name="keys_t%d" % i)
+            v_codes[i] = keep.tile([P, HEADS, HEAD], U32, name="v_codes%d" % i, align_bytes=64)
+            v_scales[i] = keep.tile([P, HEADS, HEAD], U8, name="v_scales%d" % i, align_bytes=64)
+
+        def loaded(tiles, i, h):
+            first = (h % LOAD_HEADS) * HEAD
+            return tiles[(i, h // LOAD_HEADS)][:, :, first : first + HEAD]
+
+        def prepare(i, h):
+            if i == 0:
+                decay[h] = keep.tile([P, WINDOW, PACK], F32, name="decay%d" % h)
+                nc.scalar.activation(
+                    out=decay[h][:, 0:SPAN], in_=steps[:, 0:SPAN], func=ACT.Exp, scale=math.log(gammas[h])
+                )
+            if i == 1:
+                nc.scalar.activation(
+                    out=decay[h][:, SPAN:WINDOW], in_=steps[:, SPAN:WINDOW], func=ACT.Exp, scale=math.log(gammas[h])
+                )
+            flipped = psum_flip.tile([P, 2 * PACK, P], BF16)
+            for t in range(PACK):
+                nc.tensor.transpose(flipped[:, t, :], loaded(k_raw, i, h)[:, t, :], identity[:])
+            for t in range(PACK):
+                nc.tensor.transpose(flipped[:, PACK + t, :], loaded(q_raw, i, h)[:, t, :], identity[:])
+            nc.scalar.copy(out=keys_t[i][:, h], in_=flipped[:, 0:PACK, :])
+            q_t = work.tile([P, PACK, P], BF16, bufs=AHEAD + 2)
+            nc.scalar.copy(out=q_t[:], in_=flipped[:, PACK : 2 * PACK, :])
+            queries_t[(i, h)] = q_t
+
+        def regroup_values(i, h):
+            v_side = work.tile([P, HEAD, PACK], BF16, bufs=LAG + 2, align_bytes=64)
+            nc.scalar.copy(out=v_side[:], in_=loaded(v_raw, i, h).rearrange("p t d -> p d t"))
+            v_grouped[(i, h)] = v_side
+
+        def decay_of(i, h, r, j):
+            if j == i:
+                return 1.0, decay[h][:, P * r : P * (r + 1), :]
+            return gammas[h] ** (SPAN * (i - j - 1) + P * r), decay[h][:, SPAN:WINDOW, :]
+
+        def score(s):
+            i, h, cells = rounds[s]
+            banks[s] = []
+            for e, (r, j) in enumerate(cells):
+                factor, table = decay_of(i, h, r, j)
+                cell = psum_cell.tile([P, PACK, P], F32)
+                for t in range(PACK):
+                    nc.tensor.matmul(
+                        out=cell[:, t, :],
+                        lhsT=keys_t[j][:, h, t, :],
+                        rhs=queries_t[(i, h)][:, r, :],
+                        start=True,
+                        stop=True,
+                    )
+                banks[s].append(cell)
+                if e == 0:
+                    taken_out = work.tile([P, P, PACK], F32, bufs=4)
+                    nc.scalar.mul(out=taken_out[:], in_=cell[:].rearrange("p t x -> p x t"), mul=factor)
+                    scaled[(s, e)] = taken_out
+
+        def apply_decay(s):
+            i, h, cells = rounds[s]
+            side = work.tile([P, CELLS, P, PACK], BF16, bufs=LAG + 1, align_bytes=64)
+            for e, (r, j) in enumerate(cells):
+                factor, table = decay_of(i, h, r, j)
+                if e == 0:
+                    nc.gpsimd.tensor_tensor(out=side[:, e], in0=scaled[(s, e)][:], in1=table, op=ALU.mult)
+                else:
+                    nc.vector.scalar_tensor_tensor(
+                        out=side[:, e],
+                        in0=banks[s][e][:].rearrange("p t x -> p x t"),
+                        scalar=factor,
+                        in1=table,
+                        op0=ALU.mult,
+                        op1=ALU.mult,
+                    )
+            grouped[s] = side
+
+        def quantise(s):
+            i, h, cells = rounds[s]
+            if cells[0][1] == i:
+                nc.vector.quantize_mx(
+                    out=v_codes[i][:, h, :].bitcast(FP8X4),
+                    scales=v_scales[i][:, h, :],
+                    in_=v_grouped[(i, h)][:].rearrange("p d t -> p (d t)"),
+                )
+                words = work.tile([P, CELLS, P], U32, name="diagonal_words", bufs=2, align_bytes=64)
+                plane = work.tile([P, CELLS, P], U8, name="diagonal_plane", bufs=2, align_bytes=64)
+                opening[(i, h)] = s
+            else:
+                words = work.tile([P, CELLS, P], U32, align_bytes=64)
+                plane = work.tile([P, CELLS, P], U8, align_bytes=64)
+            nc.vector.quantize_mx(
+                out=words[:].rearrange("p e x -> p (e x)").bitcast(FP8X4),
+                scales=plane[:].rearrange("p e x -> p (e x)"),
+                in_=grouped[s][:].rearrange("p e x t -> p (e x t)"),
+            )
+            codes[s], scales[s] = words, plane
+
+        def mx_pass(i, h, r, j, s, e, start, stop):
+            nc.tensor.matmul_mx(
+                out=products[(i, h)][:, r, :],
+                lhsT=codes[s][:, e, :].bitcast(FP8X4),
+                lhsT_scale=scales[s][:, e, :],
+                rhs=v_codes[j][:, h, :].bitcast(FP8X4),
+                rhs_scale=v_scales[j][:, h, :],
+                start=start,
+                stop=stop,
+            )
+
+        def multiply(s):
+            i, h, cells = rounds[s]
+            if cells[0] == (0, i):
+                product = psum_out.tile([P, PACK, HEAD], F32)
+                products[(i, h)] = product
+            for e, (r, j) in enumerate(cells):
+                if i == 0:
+                    mx_pass(i, h, r, j, s, e, True, True)
+                elif j < i:
+                    if j == 0:
+                        mx_pass(i, h, r, i, opening[(i, h)], r, True, False)
+                    mx_pass(i, h, r, j, s, e, False, j == i - 1)
+            if cells[-1] == (PACK - 1, max(i - 1, 0)):
+                result = work.tile([P, PACK, HEAD], F32)
+                nc.scalar.copy(out=result[:], in_=products[(i, h)][:])
+                nc.sync.dma_start(
+                    out=out_rows[i * SPAN : (i + 1) * SPAN, h * HEAD : (h + 1) * HEAD].rearrange(
+                        "(r p) d -> p r d", p=P
+                    ),
+                    in_=result[:],
+                )
+
+        load_span(0)
+        load_span(1)
+        for i, h in jobs[0:AHEAD]:
+            prepare(i, h)
+
+        for s in range(len(rounds) + LAG + 1):
+            if s < len(rounds):
+                score(s)
+                i, h, cells = rounds[s]
+                if cells[0] == (0, i):
+                    if h == 0 and 1 <= i < N_SPANS - 1:
+                        load_span(i + 1)
+                    regroup_values(i, h)
+                    for later in jobs[jobs.index((i, h)) + AHEAD : jobs.index((i, h)) + AHEAD + 1]:
+                        prepare(later[0], later[1])
+            if 0 <= s - LAG - 1:
+                multiply(s - LAG - 1)
+            if s < len(rounds):
+                apply_decay(s)
+            if 0 <= s - LAG < len(rounds):
+                quantise(s - LAG)

@@ -6,6 +6,7 @@ from concourse.masks import make_identity
 
 BF16 = mybir.dt.bfloat16
 F32 = mybir.dt.float32
+I32 = mybir.dt.int32
 U32 = mybir.dt.uint32
 U8 = mybir.dt.uint8
 FP8X4 = mybir.dt.float8_e4m3fn_x4
@@ -19,14 +20,31 @@ P = 128
 PACK = 4
 SPAN = P * PACK
 N_SPANS = SEQ // SPAN
+PAIRS = HEADS // 2
+QUAD = 32
+KEY_COLS = 7 * QUAD
 CELLS = 4
-LOAD_HEADS = 4
-AHEAD = 2
-WINDOW = SPAN + P
-LAG = 2
+STEP = 12
+RISE, FALL = 0, 1
+VALUE_WORDS = HEAD + HEAD // 4
 FAR = 1.0e6
+KEY_BUFS = 8
+SHIFT_BUFS = 6
+LEAD = 48
 
 FLOPS = 2 * 2 * HEAD * HEADS * SPAN * SPAN * (1 + 2 + 3 + 4)
+
+DIAGONAL = [
+    (((RISE, 0), (FALL, 2)), "three"),
+    (((RISE, 1), (FALL, 1)), "two"),
+    (((RISE, 2), (FALL, 0)), "one"),
+    (((RISE, 3),), "rise"),
+    (((FALL, 3),), "fall"),
+]
+PLACE = {
+    (RISE, 0): (0, 0), (RISE, 1): (0, 1), (FALL, 1): (0, 2), (FALL, 2): (0, 3),
+    (RISE, 2): (1, 0), (RISE, 3): (1, 1), (FALL, 0): (1, 2), (FALL, 3): (1, 3),
+}
 
 
 def tile_multiscaleretention_pa_kernel(tc, q, k, v, out):
@@ -37,202 +55,354 @@ def tile_multiscaleretention_pa_kernel(tc, q, k, v, out):
     out_rows = out.rearrange("b s h d -> (b s) (h d)")
     gammas = [1.0 - 2.0 ** (-9.0 + 4.0 * h / 7.0) for h in range(HEADS)]
 
-    jobs = [(i, h) for i in range(N_SPANS) for h in range(HEADS)]
-    rounds = []
-    for i, h in jobs:
-        rounds.append((i, h, [(r, i) for r in range(PACK)]))
-        below = [(r, j) for r in range(PACK) for j in range(i)]
-        for first in range(0, len(below), CELLS):
-            rounds.append((i, h, below[first : first + CELLS]))
+    jobs = [(a, i) for a in range(PAIRS) for i in range(N_SPANS)]
+    cells = []
+    first_cell = []
+    for n, (a, i) in enumerate(jobs):
+        first_cell.append(len(cells))
+        for strips, table in DIAGONAL:
+            cells.append((n, strips, i, table))
+            for strip in strips:
+                for j in range(i):
+                    cells.append((n, (strip,), j, "below_rise" if strip[0] == RISE else "below_fall"))
+    steps = (len(cells) + STEP - 1) // STEP
 
     with ExitStack() as stack:
         keep = stack.enter_context(tc.tile_pool(name="keep", bufs=1))
-        raw = stack.enter_context(tc.tile_pool(name="raw", bufs=2 * HEADS // LOAD_HEADS))
+        raw = stack.enter_context(tc.tile_pool(name="raw", bufs=4))
+        tables = stack.enter_context(tc.tile_pool(name="tables", bufs=2))
         work = stack.enter_context(tc.tile_pool(name="work", bufs=3))
-        psum_flip = stack.enter_context(tc.psum_pool(name="psum_flip", bufs=2))
-        psum_cell = stack.enter_context(tc.psum_pool(name="psum_cell", bufs=CELLS))
+        psum_flip = stack.enter_context(tc.psum_pool(name="psum_flip", bufs=1))
+        psum_cell = stack.enter_context(tc.psum_pool(name="psum_cell", bufs=4))
+        psum_detour = stack.enter_context(tc.psum_pool(name="psum_detour", bufs=1))
         psum_out = stack.enter_context(tc.psum_pool(name="psum_out", bufs=2))
         stack.enter_context(tc.manual_schedule())
 
-        steps = keep.tile([P, WINDOW, PACK], F32)
+        raws = {}
+
+        def load(i, half):
+            rows = slice(i * SPAN, (i + 1) * SPAN)
+            for side in (RISE, FALL):
+                cols = slice((side * PAIRS + 2 * half) * HEAD, (side * PAIRS + 2 * half + 2) * HEAD)
+                k_in = raw.tile([P, PACK, 2 * HEAD], BF16, name="k_in%d" % side)
+                nc.sync.dma_start(out=k_in[:], in_=k_rows[rows, cols].rearrange("(p t) c -> p t c", t=PACK))
+                q_in = raw.tile([P, PACK, 2 * HEAD], BF16, name="q_in%d" % side)
+                nc.sync.dma_start(out=q_in[:], in_=q_rows[rows, cols].rearrange("(t p) c -> p t c", p=P))
+                raws[("k", i, half, side)], raws[("q", i, half, side)] = k_in, q_in
+            for side in (RISE, FALL):
+                cols = slice((side * PAIRS + 2 * half) * HEAD, (side * PAIRS + 2 * half + 2) * HEAD)
+                v_in = raw.tile([P, PACK, 2 * HEAD], BF16, name="v_in%d" % side)
+                if side == RISE:
+                    nc.sync.dma_start(out=v_in[:], in_=v_rows[rows, cols].rearrange("(p t) c -> p t c", t=PACK))
+                else:
+                    for quad in range(PACK):
+                        first = i * SPAN + (PACK - 1 - quad) * P
+                        nc.sync.dma_start(
+                            out=v_in[quad * QUAD : (quad + 1) * QUAD],
+                            in_=v_rows[first : first + P, cols].rearrange("(p t) c -> p t c", t=PACK),
+                        )
+                raws[("v", i, half, side)] = v_in
+
+        def loaded(what, n, side):
+            a, i = jobs[n]
+            first = (a % 2) * HEAD
+            return raws[(what, i, a // 2, side)][:, :, first : first + HEAD]
+
+        for i in range(N_SPANS):
+            load(i, 0)
+
+        base = keep.tile([P, P, PACK], F32)
+        rise_steps = keep.tile([P, 1], F32)
+        turn = keep.tile([P, 1], F32)
+        falls = keep.tile([P, 5], F32)
+        offsets = keep.tile([P, 5], F32)
         identity = keep.tile([P, P], BF16)
+        reverse = keep.tile([P, P], BF16)
+        warm = keep.tile([P, 1], F32)
+        nc.vector.memset(warm[:], 0.0)
+        nc.scalar.activation(out=warm[:], in_=warm[:], func=ACT.Exp)
+        make_identity(nc, identity[:])
         nc.gpsimd.iota(
-            out=steps[:],
-            pattern=[[1, WINDOW], [-1, PACK]],
-            base=0,
+            out=rise_steps[:],
+            pattern=[[0, 1]],
+            base=(PACK - 1) * P,
             channel_multiplier=-PACK,
             allow_small_or_imprecise_dtypes=True,
         )
-        masked = steps[:, 0:SPAN]
-        nc.vector.scalar_tensor_tensor(out=masked, in0=masked, scalar=-FAR, in1=masked, op0=ALU.mult, op1=ALU.max)
-        make_identity(nc, identity[:])
+        nc.gpsimd.iota(
+            out=base[:],
+            pattern=[[1, P], [-1, PACK]],
+            base=0,
+            channel_multiplier=0,
+            allow_small_or_imprecise_dtypes=True,
+        )
+        nc.vector.memset(falls[:], 0.0)
+        for quad in range(PACK):
+            part = slice(quad * QUAD, (quad + 1) * QUAD)
+            nc.vector.memset(falls[part, 1 + quad : 5], 1.0)
+            nc.vector.memset(turn[part], float(P * (2 * quad - 3)))
+        for quad in range(PACK):
+            nc.vector.tensor_copy(
+                out=reverse[:, quad * QUAD : (quad + 1) * QUAD],
+                in_=identity[:, (PACK - 1 - quad) * QUAD : (PACK - quad) * QUAD],
+            )
+        nc.vector.tensor_scalar(
+            out=offsets[:], in0=falls[:], scalar1=turn[:], scalar2=rise_steps[:], op0=ALU.mult, op1=ALU.add
+        )
+        kinds = ["rise", "one", "two", "three", "fall"]
+        exponents = {}
+        for kind in ("three", "two", "one", "rise", "fall"):
+            column = offsets[:, kinds.index(kind) : kinds.index(kind) + 1]
+            plain = keep.tile([P, P, PACK], F32, name="plain_" + kind)
+            nc.vector.tensor_scalar(out=plain[:], in0=base[:], scalar1=column, scalar2=None, op0=ALU.add)
+            masked = plain
+            if kind in ("rise", "fall"):
+                exponents["below_" + kind] = plain
+                masked = keep.tile([P, P, PACK], F32, name="masked_" + kind)
+            nc.vector.scalar_tensor_tensor(
+                out=masked[:], in0=plain[:], scalar=-FAR, in1=plain[:], op0=ALU.mult, op1=ALU.max
+            )
+            exponents[kind] = masked
 
-        q_raw, k_raw, v_raw = {}, {}, {}
-        keys_t, v_codes, v_scales = {}, {}, {}
-        decay = {}
-        queries_t, v_grouped, products, opening = {}, {}, {}, {}
-        banks, grouped, codes, scales = {}, {}, {}, {}
-        scaled = {}
+        keys_t, values, shifted = [], [], []
+        for n in range(KEY_BUFS):
+            keys = keep.tile([P, 2, PACK, KEY_COLS], BF16, name="keys%d" % n)
+            nc.gpsimd.memset(keys[:].rearrange("p s t c -> p (s t c)").bitcast(I32), 0)
+            keys_t.append(keys)
+            whole = keep.tile([P, 2, VALUE_WORDS], U32, name="values%d" % n, align_bytes=64)
+            nc.gpsimd.memset(whole[:].rearrange("p s w -> p (s w)").bitcast(I32), 0)
+            values.append(whole)
+            if n < SHIFT_BUFS:
+                moved = keep.tile([P, 2, PACK - 1, VALUE_WORDS], U32, name="shifted%d" % n, align_bytes=64)
+                nc.gpsimd.memset(moved[:].rearrange("p s m w -> p (s m w)").bitcast(I32), 0)
+                shifted.append(moved)
 
-        def load_span(i):
-            rows = slice(i * SPAN, (i + 1) * SPAN)
-            for part in range(HEADS // LOAD_HEADS):
-                cols = slice(part * LOAD_HEADS * HEAD, (part + 1) * LOAD_HEADS * HEAD)
-                k_in = raw.tile([P, PACK, LOAD_HEADS * HEAD], BF16)
-                nc.sync.dma_start(out=k_in[:], in_=k_rows[rows, cols].rearrange("(p t) c -> p t c", t=PACK))
-                q_in = raw.tile([P, PACK, LOAD_HEADS * HEAD], BF16)
-                nc.sync.dma_start(out=q_in[:], in_=q_rows[rows, cols].rearrange("(t p) c -> p t c", p=P))
-                v_in = raw.tile([P, PACK, LOAD_HEADS * HEAD], BF16)
-                nc.sync.dma_start(out=v_in[:], in_=v_rows[rows, cols].rearrange("(p t) c -> p t c", t=PACK))
-                k_raw[(i, part)], q_raw[(i, part)], v_raw[(i, part)] = k_in, q_in, v_in
-            keys_t[i] = keep.tile([P, HEADS, PACK, P], BF16, name="keys_t%d" % i)
-            v_codes[i] = keep.tile([P, HEADS, HEAD], U32, name="v_codes%d" % i, align_bytes=64)
-            v_scales[i] = keep.tile([P, HEADS, HEAD], U8, name="v_scales%d" % i, align_bytes=64)
+        decay, rates, queries_t = {}, {}, {}
+        fresh_values = []
+        products = {}
+        banks, taken, side_of, codes, scales = {}, {}, {}, {}, {}
+        diagonal_of = {}
 
-        def loaded(tiles, i, h):
-            first = (h % LOAD_HEADS) * HEAD
-            return tiles[(i, h // LOAD_HEADS)][:, :, first : first + HEAD]
-
-        def prepare(i, h):
-            if i == 0:
-                decay[h] = keep.tile([P, WINDOW, PACK], F32, name="decay%d" % h)
-                nc.scalar.activation(
-                    out=decay[h][:, 0:SPAN], in_=steps[:, 0:SPAN], func=ACT.Exp, scale=math.log(gammas[h])
-                )
-            if i == 1:
-                nc.scalar.activation(
-                    out=decay[h][:, SPAN:WINDOW], in_=steps[:, SPAN:WINDOW], func=ACT.Exp, scale=math.log(gammas[h])
-                )
+        def flip(n, side):
             flipped = psum_flip.tile([P, 2 * PACK, P], BF16)
             for t in range(PACK):
-                nc.tensor.transpose(flipped[:, t, :], loaded(k_raw, i, h)[:, t, :], identity[:])
+                nc.tensor.transpose(flipped[:, t, :], loaded("k", n, side)[:, t, :], (reverse if side else identity)[:])
             for t in range(PACK):
-                nc.tensor.transpose(flipped[:, PACK + t, :], loaded(q_raw, i, h)[:, t, :], identity[:])
-            nc.scalar.copy(out=keys_t[i][:, h], in_=flipped[:, 0:PACK, :])
-            q_t = work.tile([P, PACK, P], BF16, bufs=AHEAD + 2)
+                nc.tensor.transpose(flipped[:, PACK + t, :], loaded("q", n, side)[:, t, :], identity[:])
+            first = 0 if side == FALL else 3 * QUAD
+            nc.scalar.copy(out=keys_t[n % KEY_BUFS][:, side, :, first : first + P], in_=flipped[:, 0:PACK, :])
+            q_t = work.tile([P, PACK, P], BF16, bufs=10)
             nc.scalar.copy(out=q_t[:], in_=flipped[:, PACK : 2 * PACK, :])
-            queries_t[(i, h)] = q_t
+            queries_t[(n, side)] = q_t
 
-        def regroup_values(i, h):
-            v_side = work.tile([P, HEAD, PACK], BF16, bufs=LAG + 2, align_bytes=64)
-            nc.scalar.copy(out=v_side[:], in_=loaded(v_raw, i, h).rearrange("p t d -> p d t"))
-            v_grouped[(i, h)] = v_side
-
-        def decay_of(i, h, r, j):
-            if j == i:
-                return 1.0, decay[h][:, P * r : P * (r + 1), :]
-            return gammas[h] ** (SPAN * (i - j - 1) + P * r), decay[h][:, SPAN:WINDOW, :]
-
-        def score(s):
-            i, h, cells = rounds[s]
-            banks[s] = []
-            for e, (r, j) in enumerate(cells):
-                factor, table = decay_of(i, h, r, j)
-                cell = psum_cell.tile([P, PACK, P], F32)
-                for t in range(PACK):
-                    nc.tensor.matmul(
-                        out=cell[:, t, :],
-                        lhsT=keys_t[j][:, h, t, :],
-                        rhs=queries_t[(i, h)][:, r, :],
-                        start=True,
-                        stop=True,
+        def table(n, kind):
+            a, i = jobs[n]
+            made = tables.tile([P, P, PACK], F32, name="decay_" + kind)
+            logs = [math.log(gammas[a]), math.log(gammas[a + PAIRS])]
+            if kind in ("one", "two", "three"):
+                if a not in rates:
+                    both = tables.tile([P, 5], F32, name="rates")
+                    nc.vector.tensor_scalar(
+                        out=both[:], in0=falls[:], scalar1=logs[FALL] - logs[RISE], scalar2=logs[RISE], op0=ALU.mult, op1=ALU.add
                     )
-                banks[s].append(cell)
-                if e == 0:
-                    taken_out = work.tile([P, P, PACK], F32, bufs=4)
-                    nc.scalar.mul(out=taken_out[:], in_=cell[:].rearrange("p t x -> p x t"), mul=factor)
-                    scaled[(s, e)] = taken_out
-
-        def apply_decay(s):
-            i, h, cells = rounds[s]
-            side = work.tile([P, CELLS, P, PACK], BF16, bufs=LAG + 1, align_bytes=64)
-            for e, (r, j) in enumerate(cells):
-                factor, table = decay_of(i, h, r, j)
-                if e == 0:
-                    nc.gpsimd.tensor_tensor(out=side[:, e], in0=scaled[(s, e)][:], in1=table, op=ALU.mult)
-                else:
-                    nc.vector.scalar_tensor_tensor(
-                        out=side[:, e],
-                        in0=banks[s][e][:].rearrange("p t x -> p x t"),
-                        scalar=factor,
-                        in1=table,
-                        op0=ALU.mult,
-                        op1=ALU.mult,
-                    )
-            grouped[s] = side
-
-        def quantise(s):
-            i, h, cells = rounds[s]
-            if cells[0][1] == i:
-                nc.vector.quantize_mx(
-                    out=v_codes[i][:, h, :].bitcast(FP8X4),
-                    scales=v_scales[i][:, h, :],
-                    in_=v_grouped[(i, h)][:].rearrange("p d t -> p (d t)"),
-                )
-                words = work.tile([P, CELLS, P], U32, name="diagonal_words", bufs=2, align_bytes=64)
-                plane = work.tile([P, CELLS, P], U8, name="diagonal_plane", bufs=2, align_bytes=64)
-                opening[(i, h)] = s
+                    rates[a] = both
+                rate = rates[a][:, kinds.index(kind) : kinds.index(kind) + 1]
             else:
-                words = work.tile([P, CELLS, P], U32, align_bytes=64)
-                plane = work.tile([P, CELLS, P], U8, align_bytes=64)
+                rate = logs[FALL] if kind in ("fall", "below_fall") else logs[RISE]
+            nc.scalar.activation(out=made[:], in_=exponents[kind][:], func=ACT.Exp, scale=rate)
+            decay[(a, kind)] = made
+
+        def regroup(n, side):
+            v_side = work.tile([P, HEAD, PACK], BF16, bufs=6, align_bytes=64)
+            nc.scalar.copy(out=v_side[:], in_=loaded("v", n, side).rearrange("p t d -> p d t"))
+            fresh_values.append((n, side, v_side))
+
+        def quantise_values():
+            for n, side, v_side in fresh_values:
+                whole = values[n % KEY_BUFS]
+                moved = shifted[n % SHIFT_BUFS]
+                nc.vector.quantize_mx(
+                    out=whole[:, side, 0:HEAD].bitcast(FP8X4),
+                    scales=whole[:, side, HEAD:VALUE_WORDS].bitcast(U8),
+                    in_=v_side[:].rearrange("p d t -> p (d t)"),
+                )
+                for m in range(1, PACK):
+                    low, high = slice(0, P - m * QUAD), slice(m * QUAD, P)
+                    src, dst = (low, high) if side == RISE else (high, low)
+                    nc.sync.dma_start(
+                        out=moved[dst, side, m - 1, :].bitcast(I32), in_=whole[src, side, :].bitcast(I32)
+                    )
+            fresh_values.clear()
+
+        def reload(n):
+            a, i = jobs[n]
+            if a == 1:
+                load(i, 1)
+
+        queue = []
+        for n in range(len(jobs) + 1):
+            if n < len(jobs):
+                todo = [(flip, (n, RISE)), (flip, (n, FALL))]
+                if jobs[n][1] == 0:
+                    todo += [(table, (n, kind)) for kind in ("three", "two", "one", "rise", "fall")]
+                if jobs[n][1] == 1:
+                    todo += [(table, (n, kind)) for kind in ("below_rise", "below_fall")]
+                queue += [(first_cell[n] - LEAD, call, args) for call, args in todo]
+            if n > 0:
+                todo = [(regroup, (n - 1, RISE)), (regroup, (n - 1, FALL)), (reload, (n - 1,))]
+                queue += [(first_cell[n - 1] - LEAD, call, args) for call, args in todo]
+
+        def do_chore():
+            early, call, args = queue.pop(0)
+            call(*args)
+            if queue and queue[0][1] == reload:
+                early, call, args = queue.pop(0)
+                call(*args)
+
+        def detours(c):
+            return c >= STEP and c % 3 == 2
+
+        def score(c, bank):
+            n, strips, j, kind = cells[c]
+            a, i = jobs[n]
+            keys = keys_t[(n - i + j) % KEY_BUFS]
+            for t in range(PACK):
+                for e, (side, r) in enumerate(strips):
+                    edge = r if j == i else PACK - 1
+                    first = (edge if side == RISE else PACK - 1 - edge) * QUAD
+                    nc.tensor.matmul(
+                        out=bank[:, t, :],
+                        lhsT=keys[:, side, t, first : first + P],
+                        rhs=queries_t[(n, side)][:, r, :],
+                        start=e == 0,
+                        stop=e == len(strips) - 1,
+                    )
+
+        def decay_of(c):
+            n, strips, j, kind = cells[c]
+            a, i = jobs[n]
+            if j == i:
+                return 1.0, decay[(a, kind)][:]
+            side, r = strips[0]
+            return gammas[a + side * PAIRS] ** (SPAN * (i - j) + P * r - (PACK - 1) * P), decay[(a, kind)][:]
+
+        def side_tile(c):
+            if c // CELLS not in side_of:
+                side = work.tile([P, CELLS, P, PACK], BF16, bufs=2 * STEP // CELLS, align_bytes=64)
+                side_of[c // CELLS] = side
+            return side_of[c // CELLS][:, c % CELLS]
+
+        def take_out(c):
+            bank = psum_detour.tile([P, PACK, P], F32)
+            score(c, bank)
+            factor, table_c = decay_of(c)
+            taken_out = work.tile([P, P, PACK], F32, bufs=6)
+            nc.scalar.mul(out=taken_out[:], in_=bank[:].rearrange("p t x -> p x t"), mul=factor)
+            taken[c] = taken_out
+
+        def by_gpsimd(c):
+            factor, table_c = decay_of(c)
+            nc.gpsimd.tensor_tensor(out=side_tile(c), in0=taken[c][:], in1=table_c, op=ALU.mult)
+
+        def by_vector(c):
+            bank = psum_cell.tile([P, PACK, P], F32)
+            score(c, bank)
+            factor, table_c = decay_of(c)
+            nc.vector.scalar_tensor_tensor(
+                out=side_tile(c),
+                in0=bank[:].rearrange("p t x -> p x t"),
+                scalar=factor,
+                in1=table_c,
+                op0=ALU.mult,
+                op1=ALU.mult,
+            )
+
+        def quantise(g):
+            words = work.tile([P, CELLS, P], U32, bufs=9, align_bytes=64)
+            plane = work.tile([P, CELLS, P], U8, bufs=9, align_bytes=64)
             nc.vector.quantize_mx(
                 out=words[:].rearrange("p e x -> p (e x)").bitcast(FP8X4),
                 scales=plane[:].rearrange("p e x -> p (e x)"),
-                in_=grouped[s][:].rearrange("p e x t -> p (e x t)"),
+                in_=side_of[g][:].rearrange("p e x t -> p (e x t)"),
             )
-            codes[s], scales[s] = words, plane
+            codes[g], scales[g] = words, plane
 
-        def mx_pass(i, h, r, j, s, e, start, stop):
+        def mx_pass(c, strip, start, stop):
+            n, strips, j, kind = cells[c]
+            a, i = jobs[n]
+            side, r = strip
+            bank, place = PLACE[strip]
+            if j == i and r < PACK - 1:
+                v_part = shifted[n % SHIFT_BUFS][:, side, PACK - 2 - r]
+            else:
+                v_part = values[(n - i + j) % KEY_BUFS][:, side]
             nc.tensor.matmul_mx(
-                out=products[(i, h)][:, r, :],
-                lhsT=codes[s][:, e, :].bitcast(FP8X4),
-                lhsT_scale=scales[s][:, e, :],
-                rhs=v_codes[j][:, h, :].bitcast(FP8X4),
-                rhs_scale=v_scales[j][:, h, :],
+                out=products[(n, bank)][:, place, :],
+                lhsT=codes[c // CELLS][:, c % CELLS, :].bitcast(FP8X4),
+                lhsT_scale=scales[c // CELLS][:, c % CELLS, :],
+                rhs=v_part[:, 0:HEAD].bitcast(FP8X4),
+                rhs_scale=v_part[:, HEAD:VALUE_WORDS].bitcast(U8),
                 start=start,
                 stop=stop,
             )
 
-        def multiply(s):
-            i, h, cells = rounds[s]
-            if cells[0] == (0, i):
-                product = psum_out.tile([P, PACK, HEAD], F32)
-                products[(i, h)] = product
-            for e, (r, j) in enumerate(cells):
+        def finish(n, bank):
+            a, i = jobs[n]
+            result = work.tile([P, PACK, HEAD], F32)
+            nc.scalar.copy(out=result[:], in_=products[(n, bank)][:])
+            for side in (RISE, FALL):
+                h = a + side * PAIRS
+                rows = out_rows[i * SPAN : (i + 1) * SPAN, h * HEAD : (h + 1) * HEAD].rearrange("(r p) d -> p r d", p=P)
+                if side == RISE:
+                    dst = rows[:, 2 * bank : 2 * bank + 2, :]
+                elif bank == 0:
+                    dst = rows[:, 1:3, :]
+                else:
+                    dst = rows[:, 0:4:3, :]
+                nc.sync.dma_start(out=dst, in_=result[:, 2 * side : 2 * side + 2, :])
+
+        def multiply(c):
+            n, strips, j, kind = cells[c]
+            a, i = jobs[n]
+            if j == i:
+                if (n, PLACE[strips[0]][0]) not in products:
+                    product = psum_out.tile([P, PACK, HEAD], F32)
+                    products[(n, PLACE[strips[0]][0])] = product
+                diagonal_of[n] = c
                 if i == 0:
-                    mx_pass(i, h, r, j, s, e, True, True)
-                elif j < i:
-                    if j == 0:
-                        mx_pass(i, h, r, i, opening[(i, h)], r, True, False)
-                    mx_pass(i, h, r, j, s, e, False, j == i - 1)
-            if cells[-1] == (PACK - 1, max(i - 1, 0)):
-                result = work.tile([P, PACK, HEAD], F32)
-                nc.scalar.copy(out=result[:], in_=products[(i, h)][:])
-                nc.sync.dma_start(
-                    out=out_rows[i * SPAN : (i + 1) * SPAN, h * HEAD : (h + 1) * HEAD].rearrange(
-                        "(r p) d -> p r d", p=P
-                    ),
-                    in_=result[:],
-                )
+                    for strip in strips:
+                        mx_pass(c, strip, True, True)
+            else:
+                if j == 0:
+                    mx_pass(diagonal_of[n], strips[0], True, False)
+                mx_pass(c, strips[0], False, j == i - 1)
+            if j == max(i - 1, 0) and strips[-1] in ((FALL, 1), (FALL, 3)):
+                finish(n, PLACE[strips[-1]][0])
 
-        load_span(0)
-        load_span(1)
-        for i, h in jobs[0:AHEAD]:
-            prepare(i, h)
+        for number in range(4):
+            do_chore()
 
-        for s in range(len(rounds) + LAG + 1):
-            if s < len(rounds):
-                score(s)
-                i, h, cells = rounds[s]
-                if cells[0] == (0, i):
-                    if h == 0 and 1 <= i < N_SPANS - 1:
-                        load_span(i + 1)
-                    regroup_values(i, h)
-                    for later in jobs[jobs.index((i, h)) + AHEAD : jobs.index((i, h)) + AHEAD + 1]:
-                        prepare(later[0], later[1])
-            if 0 <= s - LAG - 1:
-                multiply(s - LAG - 1)
-            if s < len(rounds):
-                apply_decay(s)
-            if 0 <= s - LAG < len(rounds):
-                quantise(s - LAG)
+        for s in range(steps + 2):
+            for slot in range(STEP):
+                c = s * STEP + slot
+                if (s == 0 or slot % 5 in (0, 3)) and queue and queue[0][0] <= c:
+                    do_chore()
+                if c < len(cells):
+                    if detours(c):
+                        by_gpsimd(c)
+                    else:
+                        by_vector(c)
+                ahead = c + STEP
+                if s > 0 and ahead < len(cells) and detours(ahead):
+                    take_out(ahead)
+                done = c - 2 * STEP
+                if 0 <= done < len(cells):
+                    multiply(done)
+            if s == 0:
+                for ahead in range(STEP, 2 * STEP):
+                    if detours(ahead):
+                        take_out(ahead)
+            for g in range((s - 1) * STEP // CELLS, s * STEP // CELLS):
+                if 0 <= g < len(cells) // CELLS:
+                    quantise(g)
+            quantise_values()

@@ -260,7 +260,7 @@ def tile_multiscaleretention_pa_kernel(tc, q, k, v, out):
                 call(*args)
 
         def detours(c):
-            return c >= STEP and c % 3 == 2
+            return c >= STEP and c % 4 == 2
 
         def score(c, bank):
             n, strips, j, kind = cells[c]

@@ -395,7 +395,7 @@ def tile_multiscaleretention_pa_kernel(tc, q, k, v, out):
                 ahead = c + STEP
                 if s > 0 and ahead < len(cells) and detours(ahead):
                     take_out(ahead)
-                done = c - 2 * STEP
+            for done in range((s - 2) * STEP, (s - 1) * STEP):
                 if 0 <= done < len(cells):
                     multiply(done)
             if s == 0:

@@ -310,9 +310,9 @@ def tile_multiscaleretention_pa_kernel(tc, q, k, v, out):
             factor, table_c = decay_of(c)
             nc.vector.scalar_tensor_tensor(
                 out=side_tile(c),
-                in0=bank[:].rearrange("p t x -> p x t"),
+                in0=table_c,
                 scalar=factor,
-                in1=table_c,
+                in1=bank[:].rearrange("p t x -> p x t"),
                 op0=ALU.mult,
                 op1=ALU.mult,
             )

@@ -72,9 +72,8 @@ def tile_multiscaleretention_pa_kernel(tc, q, k, v, out):
         raw = stack.enter_context(tc.tile_pool(name="raw", bufs=4))
         tables = stack.enter_context(tc.tile_pool(name="tables", bufs=2))
         work = stack.enter_context(tc.tile_pool(name="work", bufs=3))
-        psum_flip = stack.enter_context(tc.psum_pool(name="psum_flip", bufs=1))
+        psum_spare = stack.enter_context(tc.psum_pool(name="psum_spare", bufs=2))
         psum_cell = stack.enter_context(tc.psum_pool(name="psum_cell", bufs=4))
-        psum_detour = stack.enter_context(tc.psum_pool(name="psum_detour", bufs=1))
         psum_out = stack.enter_context(tc.psum_pool(name="psum_out", bufs=2))
         stack.enter_context(tc.manual_schedule())
 
@@ -111,6 +110,7 @@ def tile_multiscaleretention_pa_kernel(tc, q, k, v, out):
         for i in range(N_SPANS):
             load(i, 0)
 
+        rates = {}
         base = keep.tile([P, P, PACK], F32)
         rise_steps = keep.tile([P, 1], F32)
         turn = keep.tile([P, 1], F32)
@@ -121,14 +121,6 @@ def tile_multiscaleretention_pa_kernel(tc, q, k, v, out):
         warm = keep.tile([P, 1], F32)
         nc.vector.memset(warm[:], 0.0)
         nc.scalar.activation(out=warm[:], in_=warm[:], func=ACT.Exp)
-        make_identity(nc, identity[:])
-        nc.gpsimd.iota(
-            out=rise_steps[:],
-            pattern=[[0, 1]],
-            base=(PACK - 1) * P,
-            channel_multiplier=-PACK,
-            allow_small_or_imprecise_dtypes=True,
-        )
         nc.gpsimd.iota(
             out=base[:],
             pattern=[[1, P], [-1, PACK]],
@@ -136,6 +128,14 @@ def tile_multiscaleretention_pa_kernel(tc, q, k, v, out):
             channel_multiplier=0,
             allow_small_or_imprecise_dtypes=True,
         )
+        nc.gpsimd.iota(
+            out=rise_steps[:],
+            pattern=[[0, 1]],
+            base=(PACK - 1) * P,
+            channel_multiplier=-PACK,
+            allow_small_or_imprecise_dtypes=True,
+        )
+        make_identity(nc, identity[:])
         nc.vector.memset(falls[:], 0.0)
         for quad in range(PACK):
             part = slice(quad * QUAD, (quad + 1) * QUAD)
@@ -149,15 +149,25 @@ def tile_multiscaleretention_pa_kernel(tc, q, k, v, out):
         nc.vector.tensor_scalar(
             out=offsets[:], in0=falls[:], scalar1=turn[:], scalar2=rise_steps[:], op0=ALU.mult, op1=ALU.add
         )
+        for a in range(PAIRS):
+            rise_log, fall_log = math.log(gammas[a]), math.log(gammas[a + PAIRS])
+            both = keep.tile([P, 5], F32, name="rates%d" % a)
+            nc.vector.tensor_scalar(
+                out=both[:], in0=falls[:], scalar1=fall_log - rise_log, scalar2=rise_log, op0=ALU.mult, op1=ALU.add
+            )
+            rates[a] = both
         kinds = ["rise", "one", "two", "three", "fall"]
         exponents = {}
-        for kind in ("three", "two", "one", "rise", "fall"):
+        order = ("three", "two", "one", "rise", "fall")
+        for kind in order:
             column = offsets[:, kinds.index(kind) : kinds.index(kind) + 1]
             plain = keep.tile([P, P, PACK], F32, name="plain_" + kind)
             nc.vector.tensor_scalar(out=plain[:], in0=base[:], scalar1=column, scalar2=None, op0=ALU.add)
+            exponents["below_" + kind] = plain
+        for kind in order:
+            plain = exponents["below_" + kind]
             masked = plain
             if kind in ("rise", "fall"):
-                exponents["below_" + kind] = plain
                 masked = keep.tile([P, P, PACK], F32, name="masked_" + kind)
             nc.vector.scalar_tensor_tensor(
                 out=masked[:], in0=plain[:], scalar=-FAR, in1=plain[:], op0=ALU.mult, op1=ALU.max
@@ -167,24 +177,38 @@ def tile_multiscaleretention_pa_kernel(tc, q, k, v, out):
         keys_t, values, shifted = [], [], []
         for n in range(KEY_BUFS):
             keys = keep.tile([P, 2, PACK, KEY_COLS], BF16, name="keys%d" % n)
-            nc.gpsimd.memset(keys[:].rearrange("p s t c -> p (s t c)").bitcast(I32), 0)
             keys_t.append(keys)
             whole = keep.tile([P, 2, VALUE_WORDS], U32, name="values%d" % n, align_bytes=64)
-            nc.gpsimd.memset(whole[:].rearrange("p s w -> p (s w)").bitcast(I32), 0)
             values.append(whole)
             if n < SHIFT_BUFS:
                 moved = keep.tile([P, 2, PACK - 1, VALUE_WORDS], U32, name="shifted%d" % n, align_bytes=64)
-                nc.gpsimd.memset(moved[:].rearrange("p s m w -> p (s m w)").bitcast(I32), 0)
                 shifted.append(moved)
 
-        decay, rates, queries_t = {}, {}, {}
+        def zero(n):
+            empty = KEY_COLS - P
+            nc.gpsimd.memset(keys_t[n][:, RISE, :, 0:empty].bitcast(I32), 0)
+            nc.gpsimd.memset(keys_t[n][:, FALL, :, P:KEY_COLS].bitcast(I32), 0)
+
+        def zero_values(n):
+            nc.gpsimd.memset(values[n][:, :, HEAD:VALUE_WORDS].bitcast(I32), 0)
+            if n < SHIFT_BUFS:
+                nc.gpsimd.memset(shifted[n][:].rearrange("p s m w -> p (s m w)").bitcast(I32), 0)
+
+        zero(0)
+        nc.vector.memset(keys_t[1][:, RISE, 0, 0:2].bitcast(I32), 0)
+        for n in range(KEY_BUFS):
+            if n > 0:
+                zero(n)
+            zero_values(n)
+
+        decay, queries_t = {}, {}
         fresh_values = []
         products = {}
         banks, taken, side_of, codes, scales = {}, {}, {}, {}, {}
         diagonal_of = {}
 
         def flip(n, side):
-            flipped = psum_flip.tile([P, 2 * PACK, P], BF16)
+            flipped = psum_spare.tile([P, 2 * PACK, P], BF16, name="spare")
             for t in range(PACK):
                 nc.tensor.transpose(flipped[:, t, :], loaded("k", n, side)[:, t, :], (reverse if side else identity)[:])
             for t in range(PACK):
@@ -195,17 +219,14 @@ def tile_multiscaleretention_pa_kernel(tc, q, k, v, out):
             nc.scalar.copy(out=q_t[:], in_=flipped[:, PACK : 2 * PACK, :])
             queries_t[(n, side)] = q_t
 
+        def logs_of(a):
+            return math.log(gammas[a]), math.log(gammas[a + PAIRS])
+
         def table(n, kind):
             a, i = jobs[n]
             made = tables.tile([P, P, PACK], F32, name="decay_" + kind)
-            logs = [math.log(gammas[a]), math.log(gammas[a + PAIRS])]
+            logs = logs_of(a)
             if kind in ("one", "two", "three"):
-                if a not in rates:
-                    both = tables.tile([P, 5], F32, name="rates")
-                    nc.vector.tensor_scalar(
-                        out=both[:], in0=falls[:], scalar1=logs[FALL] - logs[RISE], scalar2=logs[RISE], op0=ALU.mult, op1=ALU.add
-                    )
-                    rates[a] = both
                 rate = rates[a][:, kinds.index(kind) : kinds.index(kind) + 1]
             else:
                 rate = logs[FALL] if kind in ("fall", "below_fall") else logs[RISE]
@@ -260,7 +281,7 @@ def tile_multiscaleretention_pa_kernel(tc, q, k, v, out):
                 call(*args)
 
         def detours(c):
-            return c >= STEP and c % 4 == 2
+            return STEP <= c < (steps - 1) * STEP and c % 4 == 2
 
         def score(c, bank):
             n, strips, j, kind = cells[c]
@@ -293,7 +314,7 @@ def tile_multiscaleretention_pa_kernel(tc, q, k, v, out):
             return side_of[c // CELLS][:, c % CELLS]
 
         def take_out(c):
-            bank = psum_detour.tile([P, PACK, P], F32)
+            bank = psum_spare.tile([P, PACK, P], F32, name="spare")
             score(c, bank)
             factor, table_c = decay_of(c)
             taken_out = work.tile([P, P, PACK], F32, bufs=6)
@@ -382,7 +403,18 @@ def tile_multiscaleretention_pa_kernel(tc, q, k, v, out):
         for number in range(4):
             do_chore()
 
-        for s in range(steps + 2):
+        def quantise_step(s):
+            for g in range(s * STEP // CELLS, (s + 1) * STEP // CELLS):
+                if 0 <= g < len(cells) // CELLS:
+                    quantise(g)
+
+        def multiply_step(s):
+            for c in range(max(s * STEP, 0), min((s + 1) * STEP, len(cells))):
+                multiply(c)
+
+        for s in range(steps):
+            if s == steps - 1:
+                quantise_step(s - 1)
             for slot in range(STEP):
                 c = s * STEP + slot
                 if (s == 0 or slot % 5 in (0, 3)) and queue and queue[0][0] <= c:
@@ -395,14 +427,14 @@ def tile_multiscaleretention_pa_kernel(tc, q, k, v, out):
                 ahead = c + STEP
                 if s > 0 and ahead < len(cells) and detours(ahead):
                     take_out(ahead)
-            for done in range((s - 2) * STEP, (s - 1) * STEP):
-                if 0 <= done < len(cells):
-                    multiply(done)
+            multiply_step(s - 2)
             if s == 0:
                 for ahead in range(STEP, 2 * STEP):
                     if detours(ahead):
                         take_out(ahead)
-            for g in range((s - 1) * STEP // CELLS, s * STEP // CELLS):
-                if 0 <= g < len(cells) // CELLS:
-                    quantise(g)
+            if s < steps - 1:
+                quantise_step(s - 1)
             quantise_values()
+        quantise_step(steps - 1)
+        multiply_step(steps - 2)
+        multiply_step(steps - 1)

@@ -31,6 +31,7 @@ FAR = 1.0e6
 KEY_BUFS = 8
 SHIFT_BUFS = 6
 LEAD = 48
+FIRST_LOADS = [("kq", 0), ("kq", 1), ("v", 0), ("kq", 2), ("v", 1), ("kq", 3), ("v", 2), ("v", 3)]
 
 FLOPS = 2 * 2 * HEAD * HEADS * SPAN * SPAN * (1 + 2 + 3 + 4)
 
@@ -40,6 +41,10 @@ DIAGONAL = [
     (((RISE, 2), (FALL, 0)), "one"),
     (((RISE, 3),), "rise"),
     (((FALL, 3),), "fall"),
+]
+FINISHES = [
+    (0, (FALL, 1), [(RISE, 0), (RISE, 1), (FALL, 1), (FALL, 2)]),
+    (1, (FALL, 3), [(RISE, 2), (RISE, 3), (FALL, 0), (FALL, 3)]),
 ]
 PLACE = {
     (RISE, 0): (0, 0), (RISE, 1): (0, 1), (FALL, 1): (0, 2), (FALL, 2): (0, 3),
@@ -79,10 +84,12 @@ def tile_multiscaleretention_pa_kernel(tc, q, k, v, out):
 
         raws = {}
 
-        def load(i, half):
+        def load(what, i, half):
             rows = slice(i * SPAN, (i + 1) * SPAN)
             for side in (RISE, FALL):
                 cols = slice((side * PAIRS + 2 * half) * HEAD, (side * PAIRS + 2 * half + 2) * HEAD)
+                if what == "v":
+                    break
                 k_in = raw.tile([P, PACK, 2 * HEAD], BF16, name="k_in%d" % side)
                 nc.sync.dma_start(out=k_in[:], in_=k_rows[rows, cols].rearrange("(p t) c -> p t c", t=PACK))
                 q_in = raw.tile([P, PACK, 2 * HEAD], BF16, name="q_in%d" % side)
@@ -90,6 +97,8 @@ def tile_multiscaleretention_pa_kernel(tc, q, k, v, out):
                 raws[("k", i, half, side)], raws[("q", i, half, side)] = k_in, q_in
             for side in (RISE, FALL):
                 cols = slice((side * PAIRS + 2 * half) * HEAD, (side * PAIRS + 2 * half + 2) * HEAD)
+                if what == "kq":
+                    break
                 v_in = raw.tile([P, PACK, 2 * HEAD], BF16, name="v_in%d" % side)
                 if side == RISE:
                     nc.sync.dma_start(out=v_in[:], in_=v_rows[rows, cols].rearrange("(p t) c -> p t c", t=PACK))
@@ -107,8 +116,8 @@ def tile_multiscaleretention_pa_kernel(tc, q, k, v, out):
             first = (a % 2) * HEAD
             return raws[(what, i, a // 2, side)][:, :, first : first + HEAD]
 
-        for i in range(N_SPANS):
-            load(i, 0)
+        for what, i in FIRST_LOADS:
+            load(what, i, 0)
 
         rates = {}
         base = keep.tile([P, P, PACK], F32)
@@ -196,8 +205,10 @@ def tile_multiscaleretention_pa_kernel(tc, q, k, v, out):
 
         zero(0)
         nc.vector.memset(keys_t[1][:, RISE, 0, 0:2].bitcast(I32), 0)
+        for n in range(1, PACK):
+            zero(n)
         for n in range(KEY_BUFS):
-            if n > 0:
+            if n >= PACK:
                 zero(n)
             zero_values(n)
 
@@ -258,7 +269,8 @@ def tile_multiscaleretention_pa_kernel(tc, q, k, v, out):
         def reload(n):
             a, i = jobs[n]
             if a == 1:
-                load(i, 1)
+                load("kq", i, 1)
+                load("v", i, 1)
 
         queue = []
         for n in range(len(jobs) + 1):
@@ -281,7 +293,7 @@ def tile_multiscaleretention_pa_kernel(tc, q, k, v, out):
                 call(*args)
 
         def detours(c):
-            return STEP <= c < (steps - 1) * STEP and c % 4 == 2
+            return STEP <= c < len(cells) - CELLS and c % 4 == 2
 
         def score(c, bank):
             n, strips, j, kind = cells[c]
@@ -338,21 +350,27 @@ def tile_multiscaleretention_pa_kernel(tc, q, k, v, out):
                 op1=ALU.mult,
             )
 
-        def quantise(g):
-            words = work.tile([P, CELLS, P], U32, bufs=9, align_bytes=64)
-            plane = work.tile([P, CELLS, P], U8, bufs=9, align_bytes=64)
+        def quantise(g, first=0, last=CELLS):
+            if first == 0:
+                words = work.tile([P, CELLS, P], U32, bufs=9, align_bytes=64)
+                plane = work.tile([P, CELLS, P], U8, bufs=9, align_bytes=64)
+                codes[g], scales[g] = words, plane
             nc.vector.quantize_mx(
-                out=words[:].rearrange("p e x -> p (e x)").bitcast(FP8X4),
-                scales=plane[:].rearrange("p e x -> p (e x)"),
-                in_=side_of[g][:].rearrange("p e x t -> p (e x t)"),
+                out=codes[g][:, first:last].rearrange("p e x -> p (e x)").bitcast(FP8X4),
+                scales=scales[g][:, first:last].rearrange("p e x -> p (e x)"),
+                in_=side_of[g][:, first:last].rearrange("p e x t -> p (e x t)"),
             )
-            codes[g], scales[g] = words, plane
+
+        def place_of(n, strip):
+            if (n, strip) == (len(jobs) - 1, (FALL, PACK - 1)):
+                return 2, 0
+            return PLACE[strip]
 
         def mx_pass(c, strip, start, stop):
             n, strips, j, kind = cells[c]
             a, i = jobs[n]
             side, r = strip
-            bank, place = PLACE[strip]
+            bank, place = place_of(n, strip)
             if j == i and r < PACK - 1:
                 v_part = shifted[n % SHIFT_BUFS][:, side, PACK - 2 - r]
             else:
@@ -367,28 +385,31 @@ def tile_multiscaleretention_pa_kernel(tc, q, k, v, out):
                 stop=stop,
             )
 
-        def finish(n, bank):
+        def finish(n, bank, strips):
             a, i = jobs[n]
-            result = work.tile([P, PACK, HEAD], F32)
-            nc.scalar.copy(out=result[:], in_=products[(n, bank)][:])
+            first = place_of(n, strips[0])[1]
+            result = work.tile([P, len(strips), HEAD], F32)
+            nc.scalar.copy(out=result[:], in_=products[(n, bank)][:, first : first + len(strips), :])
             for side in (RISE, FALL):
-                h = a + side * PAIRS
-                rows = out_rows[i * SPAN : (i + 1) * SPAN, h * HEAD : (h + 1) * HEAD].rearrange("(r p) d -> p r d", p=P)
-                if side == RISE:
-                    dst = rows[:, 2 * bank : 2 * bank + 2, :]
-                elif bank == 0:
-                    dst = rows[:, 1:3, :]
-                else:
-                    dst = rows[:, 0:4:3, :]
-                nc.sync.dma_start(out=dst, in_=result[:, 2 * side : 2 * side + 2, :])
+                mine = [strip for strip in strips if strip[0] == side]
+                if mine:
+                    r, step = mine[0][1], mine[-1][1] - mine[0][1] if len(mine) > 1 else 1
+                    h = a + side * PAIRS
+                    rows = out_rows[i * SPAN : (i + 1) * SPAN, h * HEAD : (h + 1) * HEAD].rearrange(
+                        "(r p) d -> p r d", p=P
+                    )
+                    place = place_of(n, mine[0])[1] - first
+                    nc.sync.dma_start(
+                        out=rows[:, r : mine[-1][1] + 1 : step, :], in_=result[:, place : place + len(mine), :]
+                    )
 
         def multiply(c):
             n, strips, j, kind = cells[c]
             a, i = jobs[n]
             if j == i:
-                if (n, PLACE[strips[0]][0]) not in products:
+                if (n, place_of(n, strips[0])[0]) not in products:
                     product = psum_out.tile([P, PACK, HEAD], F32)
-                    products[(n, PLACE[strips[0]][0])] = product
+                    products[(n, place_of(n, strips[0])[0])] = product
                 diagonal_of[n] = c
                 if i == 0:
                     for strip in strips:
@@ -397,8 +418,14 @@ def tile_multiscaleretention_pa_kernel(tc, q, k, v, out):
                 if j == 0:
                     mx_pass(diagonal_of[n], strips[0], True, False)
                 mx_pass(c, strips[0], False, j == i - 1)
-            if j == max(i - 1, 0) and strips[-1] in ((FALL, 1), (FALL, 3)):
-                finish(n, PLACE[strips[-1]][0])
+            if j == max(i - 1, 0):
+                for bank, last, done in FINISHES:
+                    if strips[-1] == last and (n < len(jobs) - 1 or bank == 0):
+                        finish(n, bank, done)
+                if n == len(jobs) - 1 and strips[0] == (RISE, 3):
+                    finish(n, 1, FINISHES[1][2][0:3])
+                if n == len(jobs) - 1 and strips[0] == (FALL, 3):
+                    finish(n, 2, FINISHES[1][2][3:4])
 
         for number in range(4):
             do_chore()
@@ -424,6 +451,13 @@ def tile_multiscaleretention_pa_kernel(tc, q, k, v, out):
                         by_gpsimd(c)
                     else:
                         by_vector(c)
+                    if c == len(cells) - 3:
+                        quantise(c // CELLS - 1)
+                    if c == len(cells) - 2:
+                        quantise(c // CELLS, 0, 2)
+                    if c == len(cells) - 1:
+                        quantise(c // CELLS, 2, 3)
+                        quantise(c // CELLS, 3, 4)
                 ahead = c + STEP
                 if s > 0 and ahead < len(cells) and detours(ahead):
                     take_out(ahead)
@@ -435,6 +469,5 @@ def tile_multiscaleretention_pa_kernel(tc, q, k, v, out):
             if s < steps - 1:
                 quantise_step(s - 1)
             quantise_values()
-        quantise_step(steps - 1)
         multiply_step(steps - 2)
         multiply_step(steps - 1)

@@ -31,6 +31,7 @@ FAR = 1.0e6
 KEY_BUFS = 8
 SHIFT_BUFS = 6
 LEAD = 48
+PARTS = (8, 4)
 FIRST_LOADS = [("kq", 0), ("kq", 1), ("v", 0), ("kq", 2), ("v", 1), ("kq", 3), ("v", 2), ("v", 3)]
 
 FLOPS = 2 * 2 * HEAD * HEADS * SPAN * SPAN * (1 + 2 + 3 + 4)
@@ -293,7 +294,7 @@ def tile_multiscaleretention_pa_kernel(tc, q, k, v, out):
                 call(*args)
 
         def detours(c):
-            return STEP <= c < len(cells) - CELLS and c % 4 == 2
+            return STEP + CELLS <= c < len(cells) - CELLS and c % 4 == 2 or c == len(cells) - CELLS
 
         def score(c, bank):
             n, strips, j, kind = cells[c]
@@ -319,11 +320,16 @@ def tile_multiscaleretention_pa_kernel(tc, q, k, v, out):
             side, r = strips[0]
             return gammas[a + side * PAIRS] ** (SPAN * (i - j) + P * r - (PACK - 1) * P), decay[(a, kind)][:]
 
+        def part_of(c):
+            s, e = c // STEP, c % STEP
+            return ((s, 0), e) if e < PARTS[0] else ((s, 1), e - PARTS[0])
+
         def side_tile(c):
-            if c // CELLS not in side_of:
-                side = work.tile([P, CELLS, P, PACK], BF16, bufs=2 * STEP // CELLS, align_bytes=64)
-                side_of[c // CELLS] = side
-            return side_of[c // CELLS][:, c % CELLS]
+            part, e = part_of(c)
+            if part not in side_of:
+                side = work.tile([P, PARTS[part[1]], P, PACK], BF16, name="side%d" % part[1], bufs=2, align_bytes=64)
+                side_of[part] = side
+            return side_of[part][:, e]
 
         def take_out(c):
             bank = psum_spare.tile([P, PACK, P], F32, name="spare")
@@ -350,15 +356,15 @@ def tile_multiscaleretention_pa_kernel(tc, q, k, v, out):
                 op1=ALU.mult,
             )
 
-        def quantise(g, first=0, last=CELLS):
+        def quantise(part, first, last):
             if first == 0:
-                words = work.tile([P, CELLS, P], U32, bufs=9, align_bytes=64)
-                plane = work.tile([P, CELLS, P], U8, bufs=9, align_bytes=64)
-                codes[g], scales[g] = words, plane
+                words = work.tile([P, PARTS[part[1]], P], U32, name="words%d" % part[1], align_bytes=64)
+                plane = work.tile([P, PARTS[part[1]], P], U8, name="plane%d" % part[1], align_bytes=64)
+                codes[part], scales[part] = words, plane
             nc.vector.quantize_mx(
-                out=codes[g][:, first:last].rearrange("p e x -> p (e x)").bitcast(FP8X4),
-                scales=scales[g][:, first:last].rearrange("p e x -> p (e x)"),
-                in_=side_of[g][:, first:last].rearrange("p e x t -> p (e x t)"),
+                out=codes[part][:, first:last].rearrange("p e x -> p (e x)").bitcast(FP8X4),
+                scales=scales[part][:, first:last].rearrange("p e x -> p (e x)"),
+                in_=side_of[part][:, first:last].rearrange("p e x t -> p (e x t)"),
             )
 
         def place_of(n, strip):
@@ -371,14 +377,15 @@ def tile_multiscaleretention_pa_kernel(tc, q, k, v, out):
             a, i = jobs[n]
             side, r = strip
             bank, place = place_of(n, strip)
+            part, e = part_of(c)
             if j == i and r < PACK - 1:
                 v_part = shifted[n % SHIFT_BUFS][:, side, PACK - 2 - r]
             else:
                 v_part = values[(n - i + j) % KEY_BUFS][:, side]
             nc.tensor.matmul_mx(
                 out=products[(n, bank)][:, place, :],
-                lhsT=codes[c // CELLS][:, c % CELLS, :].bitcast(FP8X4),
-                lhsT_scale=scales[c // CELLS][:, c % CELLS, :],
+                lhsT=codes[part][:, e, :].bitcast(FP8X4),
+                lhsT_scale=scales[part][:, e, :],
                 rhs=v_part[:, 0:HEAD].bitcast(FP8X4),
                 rhs_scale=v_part[:, HEAD:VALUE_WORDS].bitcast(U8),
                 start=start,
@@ -431,9 +438,9 @@ def tile_multiscaleretention_pa_kernel(tc, q, k, v, out):
             do_chore()
 
         def quantise_step(s):
-            for g in range(s * STEP // CELLS, (s + 1) * STEP // CELLS):
-                if 0 <= g < len(cells) // CELLS:
-                    quantise(g)
+            if 0 <= s < steps - 1:
+                quantise((s, 0), 0, PARTS[0])
+                quantise((s, 1), 0, PARTS[1])
 
         def multiply_step(s):
             for c in range(max(s * STEP, 0), min((s + 1) * STEP, len(cells))):
@@ -451,13 +458,9 @@ def tile_multiscaleretention_pa_kernel(tc, q, k, v, out):
                         by_gpsimd(c)
                     else:
                         by_vector(c)
-                    if c == len(cells) - 3:
-                        quantise(c // CELLS - 1)
-                    if c == len(cells) - 2:
-                        quantise(c // CELLS, 0, 2)
-                    if c == len(cells) - 1:
-                        quantise(c // CELLS, 2, 3)
-                        quantise(c // CELLS, 3, 4)
+                    for late, first, last in ((3, 0, 4), (2, 4, 6), (1, 6, 7), (1, 7, 8)):
+                        if c == len(cells) - late:
+                            quantise((s, 0), first, last)
                 ahead = c + STEP
                 if s > 0 and ahead < len(cells) and detours(ahead):
                     take_out(ahead)

import math
from contextlib import ExitStack

import concourse.mybir as mybir
from concourse.masks import make_identity

BF16 = mybir.dt.bfloat16
F32 = mybir.dt.float32
I32 = mybir.dt.int32
U32 = mybir.dt.uint32
U8 = mybir.dt.uint8
FP8X4 = mybir.dt.float8_e4m3fn_x4
ALU = mybir.AluOpType
ACT = mybir.ActivationFunctionType

SEQ = 2048
HEADS = 8
HEAD = 128
P = 128
PACK = 4
SPAN = P * PACK
N_SPANS = SEQ // SPAN
PAIRS = HEADS // 2
QUAD = 32
KEY_COLS = 7 * QUAD
CELLS = 4
STEP = 12
RISE, FALL = 0, 1
VALUE_WORDS = HEAD + HEAD // 4
FAR = 1.0e6
KEY_BUFS = 8
SHIFT_BUFS = 6
LEAD = 48
PARTS = (8, 4)
FIRST_LOADS = [("kq", 0), ("kq", 1), ("v", 0), ("kq", 2), ("v", 1), ("kq", 3), ("v", 2), ("v", 3)]

FLOPS = 2 * 2 * HEAD * HEADS * SPAN * SPAN * (1 + 2 + 3 + 4)

DIAGONAL = [
    (((RISE, 0), (FALL, 2)), "three"),
    (((RISE, 1), (FALL, 1)), "two"),
    (((RISE, 2), (FALL, 0)), "one"),
    (((RISE, 3),), "rise"),
    (((FALL, 3),), "fall"),
]
FINISHES = [
    (0, (FALL, 1), [(RISE, 0), (RISE, 1), (FALL, 1), (FALL, 2)]),
    (1, (FALL, 3), [(RISE, 2), (RISE, 3), (FALL, 0), (FALL, 3)]),
]
PLACE = {
    (RISE, 0): (0, 0), (RISE, 1): (0, 1), (FALL, 1): (0, 2), (FALL, 2): (0, 3),
    (RISE, 2): (1, 0), (RISE, 3): (1, 1), (FALL, 0): (1, 2), (FALL, 3): (1, 3),
}


def tile_multiscaleretention_pa_kernel(tc, q, k, v, out):
    nc = tc.nc
    q_rows = q.rearrange("b s h d -> (b s) (h d)")
    k_rows = k.rearrange("b s h d -> (b s) (h d)")
    v_rows = v.rearrange("b s h d -> (b s) (h d)")
    out_rows = out.rearrange("b s h d -> (b s) (h d)")
    gammas = [1.0 - 2.0 ** (-9.0 + 4.0 * h / 7.0) for h in range(HEADS)]

    jobs = [(a, i) for a in range(PAIRS) for i in range(N_SPANS)]
    cells = []
    first_cell = []
    for n, (a, i) in enumerate(jobs):
        first_cell.append(len(cells))
        for strips, table in DIAGONAL:
            cells.append((n, strips, i, table))
            for strip in strips:
                for j in range(i):
                    cells.append((n, (strip,), j, "below_rise" if strip[0] == RISE else "below_fall"))
    steps = (len(cells) + STEP - 1) // STEP

    with ExitStack() as stack:
        keep = stack.enter_context(tc.tile_pool(name="keep", bufs=1))
        raw = stack.enter_context(tc.tile_pool(name="raw", bufs=4))
        tables = stack.enter_context(tc.tile_pool(name="tables", bufs=2))
        work = stack.enter_context(tc.tile_pool(name="work", bufs=3))
        psum_spare = stack.enter_context(tc.psum_pool(name="psum_spare", bufs=2))
        psum_cell = stack.enter_context(tc.psum_pool(name="psum_cell", bufs=4))
        psum_out = stack.enter_context(tc.psum_pool(name="psum_out", bufs=2))
        stack.enter_context(tc.manual_schedule())

        raws = {}

        def load(what, i, half):
            rows = slice(i * SPAN, (i + 1) * SPAN)
            for side in (RISE, FALL):
                cols = slice((side * PAIRS + 2 * half) * HEAD, (side * PAIRS + 2 * half + 2) * HEAD)
                if what == "v":
                    break
                k_in = raw.tile([P, PACK, 2 * HEAD], BF16, name="k_in%d" % side)
                nc.sync.dma_start(out=k_in[:], in_=k_rows[rows, cols].rearrange("(p t) c -> p t c", t=PACK))
                q_in = raw.tile([P, PACK, 2 * HEAD], BF16, name="q_in%d" % side)
                nc.sync.dma_start(out=q_in[:], in_=q_rows[rows, cols].rearrange("(t p) c -> p t c", p=P))
                raws[("k", i, half, side)], raws[("q", i, half, side)] = k_in, q_in
            for side in (RISE, FALL):
                cols = slice((side * PAIRS + 2 * half) * HEAD, (side * PAIRS + 2 * half + 2) * HEAD)
                if what == "kq":
                    break
                v_in = raw.tile([P, PACK, 2 * HEAD], BF16, name="v_in%d" % side)
                if side == RISE:
                    nc.sync.dma_start(out=v_in[:], in_=v_rows[rows, cols].rearrange("(p t) c -> p t c", t=PACK))
                else:
                    for quad in range(PACK):
                        first = i * SPAN + (PACK - 1 - quad) * P
                        nc.sync.dma_start(
                            out=v_in[quad * QUAD : (quad + 1) * QUAD],
                            in_=v_rows[first : first + P, cols].rearrange("(p t) c -> p t c", t=PACK),
                        )
                raws[("v", i, half, side)] = v_in

        def loaded(what, n, side):
            a, i = jobs[n]
            first = (a % 2) * HEAD
            return raws[(what, i, a // 2, side)][:, :, first : first + HEAD]

        for what, i in FIRST_LOADS:
            load(what, i, 0)

        rates = {}
        base = keep.tile([P, P, PACK], F32)
        rise_steps = keep.tile([P, 1], F32)
        turn = keep.tile([P, 1], F32)
        falls = keep.tile([P, 5], F32)
        offsets = keep.tile([P, 5], F32)
        identity = keep.tile([P, P], BF16)
        reverse = keep.tile([P, P], BF16)
        warm = keep.tile([P, 1], F32)
        nc.vector.memset(warm[:], 0.0)
        nc.scalar.activation(out=warm[:], in_=warm[:], func=ACT.Exp)
        nc.gpsimd.iota(
            out=base[:],
            pattern=[[1, P], [-1, PACK]],
            base=0,
            channel_multiplier=0,
            allow_small_or_imprecise_dtypes=True,
        )
        nc.gpsimd.iota(
            out=rise_steps[:],
            pattern=[[0, 1]],
            base=(PACK - 1) * P,
            channel_multiplier=-PACK,
            allow_small_or_imprecise_dtypes=True,
        )
        make_identity(nc, identity[:])
        nc.vector.memset(falls[:], 0.0)
        for quad in range(PACK):
            part = slice(quad * QUAD, (quad + 1) * QUAD)
            nc.vector.memset(falls[part, 1 + quad : 5], 1.0)
            nc.vector.memset(turn[part], float(P * (2 * quad - 3)))
        for quad in range(PACK):
            nc.vector.tensor_copy(
                out=reverse[:, quad * QUAD : (quad + 1) * QUAD],
                in_=identity[:, (PACK - 1 - quad) * QUAD : (PACK - quad) * QUAD],
            )
        nc.vector.tensor_scalar(
            out=offsets[:], in0=falls[:], scalar1=turn[:], scalar2=rise_steps[:], op0=ALU.mult, op1=ALU.add
        )
        for a in range(PAIRS):
            rise_log, fall_log = math.log(gammas[a]), math.log(gammas[a + PAIRS])
            both = keep.tile([P, 5], F32, name="rates%d" % a)
            nc.vector.tensor_scalar(
                out=both[:], in0=falls[:], scalar1=fall_log - rise_log, scalar2=rise_log, op0=ALU.mult, op1=ALU.add
            )
            rates[a] = both
        kinds = ["rise", "one", "two", "three", "fall"]
        exponents = {}
        order = ("three", "two", "one", "rise", "fall")
        for kind in order:
            column = offsets[:, kinds.index(kind) : kinds.index(kind) + 1]
            plain = keep.tile([P, P, PACK], F32, name="plain_" + kind)
            nc.vector.tensor_scalar(out=plain[:], in0=base[:], scalar1=column, scalar2=None, op0=ALU.add)
            exponents["below_" + kind] = plain
        for kind in order:
            plain = exponents["below_" + kind]
            masked = plain
            if kind in ("rise", "fall"):
                masked = keep.tile([P, P, PACK], F32, name="masked_" + kind)
            nc.vector.scalar_tensor_tensor(
                out=masked[:], in0=plain[:], scalar=-FAR, in1=plain[:], op0=ALU.mult, op1=ALU.max
            )
            exponents[kind] = masked

        keys_t, values, shifted = [], [], []
        for n in range(KEY_BUFS):
            keys = keep.tile([P, 2, PACK, KEY_COLS], BF16, name="keys%d" % n)
            keys_t.append(keys)
            whole = keep.tile([P, 2, VALUE_WORDS], U32, name="values%d" % n, align_bytes=64)
            values.append(whole)
            if n < SHIFT_BUFS:
                moved = keep.tile([P, 2, PACK - 1, VALUE_WORDS], U32, name="shifted%d" % n, align_bytes=64)
                shifted.append(moved)

        def zero(n):
            empty = KEY_COLS - P
            nc.gpsimd.memset(keys_t[n][:, RISE, :, 0:empty].bitcast(I32), 0)
            nc.gpsimd.memset(keys_t[n][:, FALL, :, P:KEY_COLS].bitcast(I32), 0)

        def zero_values(n):
            nc.gpsimd.memset(values[n][:, :, HEAD:VALUE_WORDS].bitcast(I32), 0)
            if n < SHIFT_BUFS:
                nc.gpsimd.memset(shifted[n][:].rearrange("p s m w -> p (s m w)").bitcast(I32), 0)

        zero(0)
        nc.vector.memset(keys_t[1][:, RISE, 0, 0:2].bitcast(I32), 0)
        for n in range(1, PACK):
            zero(n)
        for n in range(KEY_BUFS):
            if n >= PACK:
                zero(n)
            zero_values(n)

        decay, queries_t = {}, {}
        fresh_values = []
        products = {}
        banks, taken, side_of, codes, scales = {}, {}, {}, {}, {}
        diagonal_of = {}

        def flip(n, side):
            flipped = psum_spare.tile([P, 2 * PACK, P], BF16, name="spare")
            for t in range(PACK):
                nc.tensor.transpose(flipped[:, t, :], loaded("k", n, side)[:, t, :], (reverse if side else identity)[:])
            for t in range(PACK):
                nc.tensor.transpose(flipped[:, PACK + t, :], loaded("q", n, side)[:, t, :], identity[:])
            first = 0 if side == FALL else 3 * QUAD
            nc.scalar.copy(out=keys_t[n % KEY_BUFS][:, side, :, first : first + P], in_=flipped[:, 0:PACK, :])
            q_t = work.tile([P, PACK, P], BF16, bufs=10)
            nc.scalar.copy(out=q_t[:], in_=flipped[:, PACK : 2 * PACK, :])
            queries_t[(n, side)] = q_t

        def logs_of(a):
            return math.log(gammas[a]), math.log(gammas[a + PAIRS])

        def table(n, kind):
            a, i = jobs[n]
            made = tables.tile([P, P, PACK], F32, name="decay_" + kind)
            logs = logs_of(a)
            if kind in ("one", "two", "three"):
                rate = rates[a][:, kinds.index(kind) : kinds.index(kind) + 1]
            else:
                rate = logs[FALL] if kind in ("fall", "below_fall") else logs[RISE]
            nc.scalar.activation(out=made[:], in_=exponents[kind][:], func=ACT.Exp, scale=rate)
            decay[(a, kind)] = made

        def regroup(n, side):
            v_side = work.tile([P, HEAD, PACK], BF16, bufs=6, align_bytes=64)
            nc.scalar.copy(out=v_side[:], in_=loaded("v", n, side).rearrange("p t d -> p d t"))
            fresh_values.append((n, side, v_side))

        def quantise_values():
            for n, side, v_side in fresh_values:
                whole = values[n % KEY_BUFS]
                moved = shifted[n % SHIFT_BUFS]
                nc.vector.quantize_mx(
                    out=whole[:, side, 0:HEAD].bitcast(FP8X4),
                    scales=whole[:, side, HEAD:VALUE_WORDS].bitcast(U8),
                    in_=v_side[:].rearrange("p d t -> p (d t)"),
                )
                for m in range(1, PACK):
                    low, high = slice(0, P - m * QUAD), slice(m * QUAD, P)
                    src, dst = (low, high) if side == RISE else (high, low)
                    nc.sync.dma_start(
                        out=moved[dst, side, m - 1, :].bitcast(I32), in_=whole[src, side, :].bitcast(I32)
                    )
            fresh_values.clear()

        def reload(n):
            a, i = jobs[n]
            if a == 1:
                load("kq", i, 1)
                load("v", i, 1)

        queue = []
        for n in range(len(jobs) + 1):
            if n < len(jobs):
                todo = [(flip, (n, RISE)), (flip, (n, FALL))]
                if jobs[n][1] == 0:
                    todo += [(table, (n, kind)) for kind in ("three", "two", "one", "rise", "fall")]
                if jobs[n][1] == 1:
                    todo += [(table, (n, kind)) for kind in ("below_rise", "below_fall")]
                queue += [(first_cell[n] - LEAD, call, args) for call, args in todo]
            if n > 0:
                todo = [(regroup, (n - 1, RISE)), (regroup, (n - 1, FALL)), (reload, (n - 1,))]
                queue += [(first_cell[n - 1] - LEAD, call, args) for call, args in todo]

        def do_chore():
            early, call, args = queue.pop(0)
            call(*args)
            if queue and queue[0][1] == reload:
                early, call, args = queue.pop(0)
                call(*args)

        def detours(c):
            return STEP + CELLS <= c < len(cells) - CELLS and c % 4 == 2 or c == len(cells) - CELLS

        def score(c, bank):
            n, strips, j, kind = cells[c]
            a, i = jobs[n]
            keys = keys_t[(n - i + j) % KEY_BUFS]
            for t in range(PACK):
                for e, (side, r) in enumerate(strips):
                    edge = r if j == i else PACK - 1
                    first = (edge if side == RISE else PACK - 1 - edge) * QUAD
                    nc.tensor.matmul(
                        out=bank[:, t, :],
                        lhsT=keys[:, side, t, first : first + P],
                        rhs=queries_t[(n, side)][:, r, :],
                        start=e == 0,
                        stop=e == len(strips) - 1,
                    )

        def decay_of(c):
            n, strips, j, kind = cells[c]
            a, i = jobs[n]
            if j == i:
                return 1.0, decay[(a, kind)][:]
            side, r = strips[0]
            return gammas[a + side * PAIRS] ** (SPAN * (i - j) + P * r - (PACK - 1) * P), decay[(a, kind)][:]

        def part_of(c):
            s, e = c // STEP, c % STEP
            return ((s, 0), e) if e < PARTS[0] else ((s, 1), e - PARTS[0])

        def side_tile(c):
            part, e = part_of(c)
            if part not in side_of:
                side = work.tile([P, PARTS[part[1]], P, PACK], BF16, name="side%d" % part[1], bufs=2, align_bytes=64)
                side_of[part] = side
            return side_of[part][:, e]

        def take_out(c):
            bank = psum_spare.tile([P, PACK, P], F32, name="spare")
            score(c, bank)
            factor, table_c = decay_of(c)
            taken_out = work.tile([P, P, PACK], F32, bufs=6)
            nc.scalar.mul(out=taken_out[:], in_=bank[:].rearrange("p t x -> p x t"), mul=factor)
            taken[c] = taken_out

        def by_gpsimd(c):
            factor, table_c = decay_of(c)
            nc.gpsimd.tensor_tensor(out=side_tile(c), in0=taken[c][:], in1=table_c, op=ALU.mult)

        def by_vector(c):
            bank = psum_cell.tile([P, PACK, P], F32)
            score(c, bank)
            factor, table_c = decay_of(c)
            nc.vector.scalar_tensor_tensor(
                out=side_tile(c),
                in0=table_c,
                scalar=factor,
                in1=bank[:].rearrange("p t x -> p x t"),
                op0=ALU.mult,
                op1=ALU.mult,
            )

        def quantise(part, first, last):
            if first == 0:
                words = work.tile([P, PARTS[part[1]], P], U32, name="words%d" % part[1], align_bytes=64)
                plane = work.tile([P, PARTS[part[1]], P], U8, name="plane%d" % part[1], align_bytes=64)
                codes[part], scales[part] = words, plane
            nc.vector.quantize_mx(
                out=codes[part][:, first:last].rearrange("p e x -> p (e x)").bitcast(FP8X4),
                scales=scales[part][:, first:last].rearrange("p e x -> p (e x)"),
                in_=side_of[part][:, first:last].rearrange("p e x t -> p (e x t)"),
            )

        def place_of(n, strip):
            if (n, strip) == (len(jobs) - 1, (FALL, PACK - 1)):
                return 2, 0
            return PLACE[strip]

        def mx_pass(c, strip, start, stop):
            n, strips, j, kind = cells[c]
            a, i = jobs[n]
            side, r = strip
            bank, place = place_of(n, strip)
            part, e = part_of(c)
            if j == i and r < PACK - 1:
                v_part = shifted[n % SHIFT_BUFS][:, side, PACK - 2 - r]
            else:
                v_part = values[(n - i + j) % KEY_BUFS][:, side]
            nc.tensor.matmul_mx(
                out=products[(n, bank)][:, place, :],
                lhsT=codes[part][:, e, :].bitcast(FP8X4),
                lhsT_scale=scales[part][:, e, :],
                rhs=v_part[:, 0:HEAD].bitcast(FP8X4),
                rhs_scale=v_part[:, HEAD:VALUE_WORDS].bitcast(U8),
                start=start,
                stop=stop,
            )

        def finish(n, bank, strips):
            a, i = jobs[n]
            first = place_of(n, strips[0])[1]
            result = work.tile([P, len(strips), HEAD], F32)
            nc.scalar.copy(out=result[:], in_=products[(n, bank)][:, first : first + len(strips), :])
            for side in (RISE, FALL):
                mine = [strip for strip in strips if strip[0] == side]
                if mine:
                    r, step = mine[0][1], mine[-1][1] - mine[0][1] if len(mine) > 1 else 1
                    h = a + side * PAIRS
                    rows = out_rows[i * SPAN : (i + 1) * SPAN, h * HEAD : (h + 1) * HEAD].rearrange(
                        "(r p) d -> p r d", p=P
                    )
                    place = place_of(n, mine[0])[1] - first
                    nc.sync.dma_start(
                        out=rows[:, r : mine[-1][1] + 1 : step, :], in_=result[:, place : place + len(mine), :]
                    )

        def multiply(c):
            n, strips, j, kind = cells[c]
            a, i = jobs[n]
            if j == i:
                if (n, place_of(n, strips[0])[0]) not in products:
                    product = psum_out.tile([P, PACK, HEAD], F32)
                    products[(n, place_of(n, strips[0])[0])] = product
                diagonal_of[n] = c
                if i == 0:
                    for strip in strips:
                        mx_pass(c, strip, True, True)
            else:
                if j == 0:
                    mx_pass(diagonal_of[n], strips[0], True, False)
                mx_pass(c, strips[0], False, j == i - 1)
            if j == max(i - 1, 0):
                for bank, last, done in FINISHES:
                    if strips[-1] == last and (n < len(jobs) - 1 or bank == 0):
                        finish(n, bank, done)
                if n == len(jobs) - 1 and strips[0] == (RISE, 3):
                    finish(n, 1, FINISHES[1][2][0:3])
                if n == len(jobs) - 1 and strips[0] == (FALL, 3):
                    finish(n, 2, FINISHES[1][2][3:4])

        for number in range(4):
            do_chore()

        def quantise_step(s):
            if 0 <= s < steps - 1:
                quantise((s, 0), 0, PARTS[0])
                quantise((s, 1), 0, PARTS[1])

        def multiply_step(s):
            for c in range(max(s * STEP, 0), min((s + 1) * STEP, len(cells))):
                multiply(c)

        for s in range(steps):
            if s == steps - 1:
                quantise_step(s - 1)
            for slot in range(STEP):
                c = s * STEP + slot
                if (s == 0 or slot % 5 in (0, 3)) and queue and queue[0][0] <= c:
                    do_chore()
                if c < len(cells):
                    if detours(c):
                        by_gpsimd(c)
                    else:
                        by_vector(c)
                    for late, first, last in ((3, 0, 4), (2, 4, 6), (1, 6, 7), (1, 7, 8)):
                        if c == len(cells) - late:
                            quantise((s, 0), first, last)
                ahead = c + STEP
                if s > 0 and ahead < len(cells) and detours(ahead):
                    take_out(ahead)
            multiply_step(s - 2)
            if s == 0:
                for ahead in range(STEP, 2 * STEP):
                    if detours(ahead):
                        take_out(ahead)
            if s < steps - 1:
                quantise_step(s - 1)
            quantise_values()
        multiply_step(steps - 2)
        multiply_step(steps - 1)
